import numpy as np
import ml_dtypes


def mxq(x, axis, fmt="e4m3"):
    dtype, down = {"e4m3": (ml_dtypes.float8_e4m3fn, 7), "e5m2": (ml_dtypes.float8_e5m2, 14)}[fmt]
    v = np.moveaxis(np.asarray(x, np.float32).astype(ml_dtypes.bfloat16).astype(np.float64), axis, -1)
    blocks = v.reshape(v.shape[:-1] + (-1, 32))
    amax = np.abs(blocks).max(-1, keepdims=True)
    byte = np.maximum(np.where(amax > 0, np.frexp(amax)[1] - 1 + 127, 0) - down, 1)
    scale = np.exp2(byte - 127.0)
    codes = (blocks / scale).astype(np.float32).astype(dtype).astype(np.float64)
    return np.moveaxis((codes * scale).reshape(v.shape), -1, axis)


WIDE = False


def mx_kscale(k):
    if not WIDE:
        return np.ones(k)
    levels = np.array([10, -10, 5, -5, 0])
    a = np.random.permutation(np.resize(levels, k // 512 * 4)).reshape(k // 512, 4)
    idx = np.arange(k)
    return np.exp2(a[idx // 512, idx % 128 // 32])


BF16 = ml_dtypes.bfloat16


def bf(x):
    return np.asarray(x, np.float32).astype(BF16)


def f64(x):
    return np.asarray(x).astype(np.float64)


W, S, K, T, D = 4, 256, 4, 128, 1024
LN_EPS = 1e-5


def layer_norm(x, gamma, beta):
    mu = x.mean(-1, keepdims=True)
    var = np.square(x - mu).mean(-1, keepdims=True)
    return (x - mu) / np.sqrt(var + LN_EPS) * gamma + beta


def setup_inputs():
    n = np.random.standard_normal
    s = mx_kscale(D)
    shot_bias = np.repeat(np.log(np.random.uniform(0.05, 1.0, (W, K))), T, axis=1)
    return {"logits": bf(n((W, S, K * T)) * 1.5 + shot_bias[:, None, :]),
            "support_transport": bf(n((W, K, T, D)) * s),
            "Wv": bf(n((D, D)) * 1.5 / np.sqrt(D) / s[None, :]),
            "class_slots": bf(n((W, S, D)) * 0.5),
            "g_out": bf(1.0 + 0.1 * n(D)),
            "b_out": bf(0.1 * n(D))}


def reference(logits, support_transport, Wv, class_slots, g_out, b_out):
    flat = f64(support_transport).reshape(W, K * T, D)
    v = mxq(flat, 2, "e4m3") @ mxq(f64(Wv), 1, "e4m3").T
    l = f64(logits)
    e = np.exp(l - l.max(-1, keepdims=True))
    mem = (mxq(e, 2, "e4m3") @ mxq(v, 1, "e4m3")) / e.sum(-1, keepdims=True)
    return layer_norm(f64(class_slots) + mem, f64(g_out), f64(b_out))

@@ -1,0 +1,240 @@
+from contextlib import ExitStack
+
+import concourse.mybir as mybir
+from concourse.masks import make_identity
+
+FP8X4 = mybir.dt.float8_e4m3fn_x4
+BF16 = mybir.dt.bfloat16
+F32 = mybir.dt.float32
+U32 = mybir.dt.uint32
+U8 = mybir.dt.uint8
+ACT = mybir.ActivationFunctionType
+ALU = mybir.AluOpType
+AXIS = mybir.AxisListType
+
+P = 128
+PACK = 4
+CLASSES = 4
+SLOTS = 256
+TOKENS = 512
+FEATURES = 1024
+LN_EPS = 1e-5
+
+SLOT_TILES = SLOTS // P
+K_PASSES = FEATURES // (P * PACK)
+WORDS = FEATURES // 2
+OUT_TILES = FEATURES // P
+HALF = 512
+HALVES = FEATURES // HALF
+
+FLOPS = 2 * CLASSES * TOKENS * FEATURES * FEATURES + 2 * CLASSES * SLOTS * TOKENS * FEATURES
+
+
+def tile_consensustransportmemorypool_pb_kernel(
+    tc, logits, support_transport, Wv, class_slots, g_out, b_out, out
+):
+    nc = tc.nc
+    with ExitStack() as stack:
+        consts = stack.enter_context(tc.tile_pool(name="consts", bufs=1))
+        inputs = stack.enter_context(tc.tile_pool(name="inputs", bufs=1))
+        keep = stack.enter_context(tc.tile_pool(name="keep", bufs=1))
+        stage = stack.enter_context(tc.tile_pool(name="stage", bufs=2))
+        rows = stack.enter_context(tc.tile_pool(name="rows", bufs=4))
+        stats = stack.enter_context(tc.tile_pool(name="stats", bufs=4))
+        psum_t = stack.enter_context(tc.psum_pool(name="psum_t", bufs=3))
+        psum_v = stack.enter_context(tc.psum_pool(name="psum_v", bufs=3))
+        psum_mem = stack.enter_context(tc.psum_pool(name="psum_mem", bufs=2))
+
+        logit_rows = inputs.tile([P, CLASSES, SLOT_TILES, TOKENS], BF16)
+        flat_rows = [inputs.tile([P, PACK * FEATURES], BF16, name="flat_rows%d" % w) for w in range(CLASSES)]
+        wv_rows = inputs.tile([P, OUT_TILES * FEATURES], BF16)
+        slot_rows = [inputs.tile([P, SLOT_TILES, FEATURES], BF16, name="slot_rows%d" % w) for w in range(CLASSES)]
+        gain = consts.tile([P, FEATURES], BF16)
+        shift = consts.tile([P, FEATURES], BF16)
+
+        def load_flat(w):
+            tokens = support_transport[w].rearrange("k t d -> (k t) d")
+            nc.sync.dma_start(
+                out=flat_rows[w][:].rearrange("p (j d) -> p j d", j=PACK),
+                in_=tokens.rearrange("(p j) d -> p j d", j=PACK),
+            )
+
+        def load_slots(w):
+            nc.sync.dma_start(out=slot_rows[w][:], in_=class_slots[w].rearrange("(p i) d -> p i d", i=SLOT_TILES))
+
+        for w in range(CLASSES):
+            nc.sync.dma_start(out=logit_rows[:, w], in_=logits[w].rearrange("(p i) t -> p i t", i=SLOT_TILES))
+        load_flat(0)
+        wv_tiles = Wv.rearrange("(c p) k -> p c k", p=P)
+        wv_rows_by_tile = wv_rows[:].rearrange("p (c k) -> p c k", c=OUT_TILES)
+        for c in range(0, OUT_TILES, 2):
+            nc.sync.dma_start(out=wv_rows_by_tile[:, c : c + 2, :], in_=wv_tiles[:, c : c + 2, :])
+        load_flat(1)
+        load_slots(0)
+        nc.sync.dma_start(out=gain[:], in_=g_out.partition_broadcast(P))
+        nc.sync.dma_start(out=shift[:], in_=b_out.partition_broadcast(P))
+        load_flat(2)
+        load_slots(1)
+        load_flat(3)
+        load_slots(2)
+        load_slots(3)
+
+        ident_f32 = consts.tile([P, P], F32)
+        make_identity(nc, ident_f32[:])
+        ident_bf16 = consts.tile([P, P], BF16)
+        make_identity(nc, ident_bf16[:])
+        eps = consts.tile([P, 1], F32)
+        nc.vector.memset(eps[:], LN_EPS)
+
+        neg_max = keep.tile([P, CLASSES, SLOT_TILES], F32)
+        e_sum = keep.tile([P, CLASSES, SLOT_TILES], F32)
+        inv_sum = keep.tile([P, CLASSES, SLOT_TILES], F32)
+        e_rows = keep.tile([P, CLASSES, SLOT_TILES, TOKENS], BF16)
+        e_codes = keep.tile([P, CLASSES, SLOTS], U32, align_bytes=64)
+        e_scales = keep.tile([P, CLASSES, SLOTS], U8, align_bytes=64)
+
+        def softmax_numerators(w):
+            nc.vector.tensor_reduce(out=neg_max[:, w, :], in_=logit_rows[:, w], axis=AXIS.X, op=ALU.max, negate=True)
+            for i in range(SLOT_TILES):
+                nc.scalar.activation(
+                    out=e_rows[:, w, i, :],
+                    in_=logit_rows[:, w, i, :],
+                    func=ACT.Exp,
+                    bias=neg_max[:, w, i : i + 1],
+                    scale=1.0,
+                    accum_out=e_sum[:, w, i : i + 1],
+                )
+            nc.vector.reciprocal(out=inv_sum[:, w, :], in_=e_sum[:, w, :])
+
+        def quantise_e(w):
+            e_t = psum_t.tile([P, PACK, SLOTS], BF16, tag="t")
+            for i in range(SLOT_TILES):
+                every_fourth = e_rows[:, w, i, :].rearrange("s (p j) -> s j p", j=PACK)
+                for j in range(PACK):
+                    nc.tensor.transpose(e_t[:, j, i * P : (i + 1) * P], every_fourth[:, j, :], ident_bf16[:])
+            e_grouped = stage.tile([P, SLOTS, PACK], BF16, align_bytes=64)
+            nc.vector.tensor_copy(out=e_grouped[:], in_=e_t[:].rearrange("p j s -> p s j"))
+            nc.vector.quantize_mx(
+                out=e_codes[:, w, :].bitcast(FP8X4),
+                scales=e_scales[:, w, :],
+                in_=e_grouped[:].rearrange("p s j -> p (s j)"),
+            )
+
+        def transpose_row_tile(words, grouped_words):
+            x_t = psum_t.tile([P, K_PASSES, 2, P], F32, tag="t")
+            for g in range(K_PASSES):
+                for u in range(2):
+                    first = (2 * g + u) * P
+                    nc.tensor.transpose(x_t[:, g, u, :], words[:, first : first + P], ident_f32[:])
+            nc.scalar.copy(
+                out=grouped_words.rearrange("p (g r u) -> p g r u", g=K_PASSES, u=2),
+                in_=x_t[:].rearrange("p g u r -> p g r u"),
+            )
+
+        def quantise_flat(w):
+            words = flat_rows[w][:].bitcast(F32)
+            flat_grouped = stage.tile([P, PACK * FEATURES], BF16, align_bytes=64)
+            grouped_words = flat_grouped[:].bitcast(F32)
+            for j in range(PACK):
+                transpose_row_tile(words[:, j * WORDS : (j + 1) * WORDS], grouped_words[:, j * WORDS : (j + 1) * WORDS])
+            flat_codes = stage.tile([P, PACK * K_PASSES * P], U32, align_bytes=64)
+            flat_scales = stage.tile([P, PACK * K_PASSES * P], U8, align_bytes=64)
+            nc.vector.quantize_mx(out=flat_codes[:].bitcast(FP8X4), scales=flat_scales[:], in_=flat_grouped[:])
+            return flat_codes, flat_scales
+
+        wv_codes = keep.tile([P, OUT_TILES * K_PASSES * P], U32, align_bytes=64)
+        wv_scales = keep.tile([P, OUT_TILES * K_PASSES * P], U8, align_bytes=64)
+
+        def quantise_wv(c):
+            words = wv_rows[:].bitcast(F32)
+            wv_grouped = stage.tile([P, FEATURES], BF16, align_bytes=64)
+            transpose_row_tile(words[:, c * WORDS : (c + 1) * WORDS], wv_grouped[:].bitcast(F32))
+            cols = slice(c * K_PASSES * P, (c + 1) * K_PASSES * P)
+            nc.vector.quantize_mx(out=wv_codes[:, cols].bitcast(FP8X4), scales=wv_scales[:, cols], in_=wv_grouped[:])
+
+        def project(flat_codes, flat_scales, c, v_grouped):
+            v_acc = psum_v.tile([P, PACK, P], F32)
+            for j in range(PACK):
+                for g in range(K_PASSES):
+                    tok = slice((j * K_PASSES + g) * P, (j * K_PASSES + g + 1) * P)
+                    col = slice((c * K_PASSES + g) * P, (c * K_PASSES + g + 1) * P)
+                    nc.tensor.matmul_mx(
+                        out=v_acc[:, j, :],
+                        lhsT=flat_codes[:, tok].bitcast(FP8X4),
+                        lhsT_scale=flat_scales[:, tok],
+                        rhs=wv_codes[:, col].bitcast(FP8X4),
+                        rhs_scale=wv_scales[:, col],
+                        start=(g == 0),
+                        stop=(g == K_PASSES - 1),
+                    )
+            nc.scalar.copy(out=v_grouped[:, c * P : (c + 1) * P, :], in_=v_acc[:].rearrange("p j c -> p c j"))
+
+        def pool_half(w, i, h, v_codes, v_scales, y, y_sum):
+            cols = slice(h * HALF, (h + 1) * HALF)
+            slots = slice(i * P, (i + 1) * P)
+            mem = psum_mem.tile([P, HALF], F32)
+            nc.tensor.matmul_mx(
+                out=mem[:],
+                lhsT=e_codes[:, w, slots].bitcast(FP8X4),
+                lhsT_scale=e_scales[:, w, slots],
+                rhs=v_codes[:, cols].bitcast(FP8X4),
+                rhs_scale=v_scales[:, cols],
+                start=True,
+                stop=True,
+            )
+            nc.vector.scalar_tensor_tensor(
+                out=y[:, cols],
+                in0=mem[:],
+                scalar=inv_sum[:, w, i : i + 1],
+                in1=slot_rows[w][:, i, cols],
+                op0=ALU.mult,
+                op1=ALU.add,
+                accum_out=y_sum[:, h : h + 1],
+            )
+
+        def layer_norm(w, i, y, y_sum):
+            neg_mean = stats.tile([P, 1], F32)
+            nc.vector.tensor_scalar(
+                out=neg_mean[:], in0=y_sum[:, 0:1], scalar1=y_sum[:, 1:2], scalar2=-1.0 / FEATURES, op0=ALU.add, op1=ALU.mult
+            )
+            squares = stage.tile([P, FEATURES], BF16)
+            sum_sq = stats.tile([P, 1], F32)
+            nc.scalar.activation(out=squares[:], in_=y[:], func=ACT.Square, bias=neg_mean[:], scale=1.0, accum_out=sum_sq[:])
+            z = rows.tile([P, FEATURES], F32)
+            nc.vector.scalar_tensor_tensor(out=z[:], in0=y[:], scalar=neg_mean[:], in1=gain[:], op0=ALU.add, op1=ALU.mult)
+            std = stats.tile([P, 1], F32)
+            nc.scalar.activation(out=std[:], in_=sum_sq[:], func=ACT.Sqrt, bias=eps[:], scale=1.0 / FEATURES)
+            inv_std = stats.tile([P, 1], F32)
+            nc.vector.reciprocal(out=inv_std[:], in_=std[:])
+            nc.vector.scalar_tensor_tensor(out=z[:], in0=z[:], scalar=inv_std[:], in1=shift[:], op0=ALU.mult, op1=ALU.add)
+            nc.sync.dma_start(out=out[w].rearrange("(p i) d -> p i d", i=SLOT_TILES)[:, i, :], in_=z[:])
+
+        for w in range(CLASSES):
+            softmax_numerators(w)
+        for w in range(CLASSES):
+            quantise_e(w)
+        flat_mx = {0: quantise_flat(0)}
+        for c in range(OUT_TILES):
+            quantise_wv(c)
+        for w in range(CLASSES):
+            flat_codes, flat_scales = flat_mx[w]
+            v_grouped = stage.tile([P, FEATURES, PACK], BF16, align_bytes=64)
+            v_codes = stage.tile([P, FEATURES], U32, align_bytes=64)
+            v_scales = stage.tile([P, FEATURES], U8, align_bytes=64)
+            y_rows = [rows.tile([P, FEATURES], F32, name="y") for i in range(SLOT_TILES)]
+            y_sums = [stats.tile([P, HALVES], F32, name="y_sum") for i in range(SLOT_TILES)]
+            for h in range(HALVES):
+                for c in range(h * OUT_TILES // HALVES, (h + 1) * OUT_TILES // HALVES):
+                    project(flat_codes, flat_scales, c, v_grouped)
+                if h == 0 and w + 1 < CLASSES:
+                    flat_mx[w + 1] = quantise_flat(w + 1)
+                cols = slice(h * HALF, (h + 1) * HALF)
+                nc.vector.quantize_mx(
+                    out=v_codes[:, cols].bitcast(FP8X4),
+                    scales=v_scales[:, cols],
+                    in_=v_grouped[:, cols, :].rearrange("p c j -> p (c j)"),
+                )
+                for i in range(SLOT_TILES):
+                    pool_half(w, i, h, v_codes, v_scales, y_rows[i], y_sums[i])
+            for i in range(SLOT_TILES):
+                layer_norm(w, i, y_rows[i], y_sums[i])

@@ -27,6 +27,10 @@ OUT_TILES = FEATURES // P
 HALF = 512
 HALVES = FEATURES // HALF
 
+S_BANKS = 6
+M_BANKS = 2
+WV_RUN = 4
+
 FLOPS = 2 * CLASSES * TOKENS * FEATURES * FEATURES + 2 * CLASSES * SLOTS * TOKENS * FEATURES
 
 
@@ -41,9 +45,9 @@ def tile_consensustransportmemorypool_pb_kernel(
         stage = stack.enter_context(tc.tile_pool(name="stage", bufs=2))
         rows = stack.enter_context(tc.tile_pool(name="rows", bufs=4))
         stats = stack.enter_context(tc.tile_pool(name="stats", bufs=4))
-        psum_t = stack.enter_context(tc.psum_pool(name="psum_t", bufs=3))
-        psum_v = stack.enter_context(tc.psum_pool(name="psum_v", bufs=3))
-        psum_mem = stack.enter_context(tc.psum_pool(name="psum_mem", bufs=2))
+        psum_s = stack.enter_context(tc.psum_pool(name="psum_s", bufs=S_BANKS))
+        psum_m = stack.enter_context(tc.psum_pool(name="psum_m", bufs=M_BANKS))
+        stack.enter_context(tc.manual_schedule())
 
         logit_rows = inputs.tile([P, CLASSES, SLOT_TILES, TOKENS], BF16)
         flat_rows = [inputs.tile([P, PACK * FEATURES], BF16, name="flat_rows%d" % w) for w in range(CLASSES)]
@@ -92,6 +96,7 @@ def tile_consensustransportmemorypool_pb_kernel(
         e_rows = keep.tile([P, CLASSES, SLOT_TILES, TOKENS], BF16)
         e_codes = keep.tile([P, CLASSES, SLOTS], U32, align_bytes=64)
         e_scales = keep.tile([P, CLASSES, SLOTS], U8, align_bytes=64)
+        e_banks = {}
 
         def softmax_numerators(w):
             nc.vector.tensor_reduce(out=neg_max[:, w, :], in_=logit_rows[:, w], axis=AXIS.X, op=ALU.max, negate=True)
@@ -104,16 +109,19 @@ def tile_consensustransportmemorypool_pb_kernel(
                     scale=1.0,
                     accum_out=e_sum[:, w, i : i + 1],
                 )
-            nc.vector.reciprocal(out=inv_sum[:, w, :], in_=e_sum[:, w, :])
 
-        def quantise_e(w):
-            e_t = psum_t.tile([P, PACK, SLOTS], BF16, tag="t")
+        def transpose_e(w):
+            e_t = psum_m.tile([P, PACK, SLOTS], BF16, tag="m")
             for i in range(SLOT_TILES):
                 every_fourth = e_rows[:, w, i, :].rearrange("s (p j) -> s j p", j=PACK)
                 for j in range(PACK):
                     nc.tensor.transpose(e_t[:, j, i * P : (i + 1) * P], every_fourth[:, j, :], ident_bf16[:])
+            e_banks[w] = e_t
+
+        def quantise_e(w):
             e_grouped = stage.tile([P, SLOTS, PACK], BF16, align_bytes=64)
-            nc.vector.tensor_copy(out=e_grouped[:], in_=e_t[:].rearrange("p j s -> p s j"))
+            nc.vector.tensor_copy(out=e_grouped[:], in_=e_banks[w][:].rearrange("p j s -> p s j"))
+            nc.vector.reciprocal(out=inv_sum[:, w, :], in_=e_sum[:, w, :])
             nc.vector.quantize_mx(
                 out=e_codes[:, w, :].bitcast(FP8X4),
                 scales=e_scales[:, w, :],
@@ -121,7 +129,7 @@ def tile_consensustransportmemorypool_pb_kernel(
             )
 
         def transpose_row_tile(words, grouped_words):
-            x_t = psum_t.tile([P, K_PASSES, 2, P], F32, tag="t")
+            x_t = psum_s.tile([P, K_PASSES, 2, P], F32, tag="s")
             for g in range(K_PASSES):
                 for u in range(2):
                     first = (2 * g + u) * P
@@ -131,29 +139,56 @@ def tile_consensustransportmemorypool_pb_kernel(
                 in_=x_t[:].rearrange("p g u r -> p g r u"),
             )
 
-        def quantise_flat(w):
+        flat_grouped = {}
+        flat_mx = {}
+
+        def transpose_flat(w):
+            flat_grouped[w] = stage.tile([P, PACK * FEATURES], BF16, align_bytes=64, name="flat_grouped")
             words = flat_rows[w][:].bitcast(F32)
-            flat_grouped = stage.tile([P, PACK * FEATURES], BF16, align_bytes=64)
-            grouped_words = flat_grouped[:].bitcast(F32)
+            grouped_words = flat_grouped[w][:].bitcast(F32)
             for j in range(PACK):
                 transpose_row_tile(words[:, j * WORDS : (j + 1) * WORDS], grouped_words[:, j * WORDS : (j + 1) * WORDS])
+
+        def quantise_flat(w):
             flat_codes = stage.tile([P, PACK * K_PASSES * P], U32, align_bytes=64)
             flat_scales = stage.tile([P, PACK * K_PASSES * P], U8, align_bytes=64)
-            nc.vector.quantize_mx(out=flat_codes[:].bitcast(FP8X4), scales=flat_scales[:], in_=flat_grouped[:])
-            return flat_codes, flat_scales
+            nc.vector.quantize_mx(out=flat_codes[:].bitcast(FP8X4), scales=flat_scales[:], in_=flat_grouped[w][:])
+            flat_mx[w] = (flat_codes, flat_scales)
 
         wv_codes = keep.tile([P, OUT_TILES * K_PASSES * P], U32, align_bytes=64)
         wv_scales = keep.tile([P, OUT_TILES * K_PASSES * P], U8, align_bytes=64)
 
-        def quantise_wv(c):
-            words = wv_rows[:].bitcast(F32)
-            wv_grouped = stage.tile([P, FEATURES], BF16, align_bytes=64)
-            transpose_row_tile(words[:, c * WORDS : (c + 1) * WORDS], wv_grouped[:].bitcast(F32))
-            cols = slice(c * K_PASSES * P, (c + 1) * K_PASSES * P)
-            nc.vector.quantize_mx(out=wv_codes[:, cols].bitcast(FP8X4), scales=wv_scales[:, cols], in_=wv_grouped[:])
+        wv_grouped = keep.tile([P, OUT_TILES * FEATURES], BF16, align_bytes=64)
 
-        def project(flat_codes, flat_scales, c, v_grouped):
-            v_acc = psum_v.tile([P, PACK, P], F32)
+        def transpose_wv(c):
+            words = wv_rows[:].bitcast(F32)
+            grouped_words = wv_grouped[:].bitcast(F32)
+            transpose_row_tile(words[:, c * WORDS : (c + 1) * WORDS], grouped_words[:, c * WORDS : (c + 1) * WORDS])
+
+        def quantise_wv(first, count):
+            nc.vector.quantize_mx(
+                out=wv_codes[:, first * K_PASSES * P : (first + count) * K_PASSES * P].bitcast(FP8X4),
+                scales=wv_scales[:, first * K_PASSES * P : (first + count) * K_PASSES * P],
+                in_=wv_grouped[:, first * FEATURES : (first + count) * FEATURES],
+            )
+
+        v_grouped = {}
+        v_mx = {}
+        y_rows = {}
+        y_sums = {}
+
+        def open_class(w):
+            v_grouped[w] = stage.tile([P, FEATURES, PACK], BF16, align_bytes=64, name="v_grouped")
+            v_codes = stage.tile([P, FEATURES], U32, align_bytes=64)
+            v_scales = stage.tile([P, FEATURES], U8, align_bytes=64)
+            v_mx[w] = (v_codes, v_scales)
+            for i in range(SLOT_TILES):
+                y_rows[w, i] = rows.tile([P, FEATURES], F32, name="y")
+                y_sums[w, i] = stats.tile([P, HALVES], F32, name="y_sum")
+
+        def project(w, c):
+            flat_codes, flat_scales = flat_mx[w]
+            v_acc = psum_s.tile([P, PACK, P], F32, tag="s")
             for j in range(PACK):
                 for g in range(K_PASSES):
                     tok = slice((j * K_PASSES + g) * P, (j * K_PASSES + g + 1) * P)
@@ -167,74 +202,119 @@ def tile_consensustransportmemorypool_pb_kernel(
                         start=(g == 0),
                         stop=(g == K_PASSES - 1),
                     )
-            nc.scalar.copy(out=v_grouped[:, c * P : (c + 1) * P, :], in_=v_acc[:].rearrange("p j c -> p c j"))
+            nc.scalar.copy(out=v_grouped[w][:, c * P : (c + 1) * P, :], in_=v_acc[:].rearrange("p j c -> p c j"))
 
-        def pool_half(w, i, h, v_codes, v_scales, y, y_sum):
+        def quantise_v(w, h):
+            v_codes, v_scales = v_mx[w]
             cols = slice(h * HALF, (h + 1) * HALF)
-            slots = slice(i * P, (i + 1) * P)
-            mem = psum_mem.tile([P, HALF], F32)
-            nc.tensor.matmul_mx(
-                out=mem[:],
-                lhsT=e_codes[:, w, slots].bitcast(FP8X4),
-                lhsT_scale=e_scales[:, w, slots],
-                rhs=v_codes[:, cols].bitcast(FP8X4),
-                rhs_scale=v_scales[:, cols],
-                start=True,
-                stop=True,
-            )
-            nc.vector.scalar_tensor_tensor(
-                out=y[:, cols],
-                in0=mem[:],
-                scalar=inv_sum[:, w, i : i + 1],
-                in1=slot_rows[w][:, i, cols],
-                op0=ALU.mult,
-                op1=ALU.add,
-                accum_out=y_sum[:, h : h + 1],
+            nc.vector.quantize_mx(
+                out=v_codes[:, cols].bitcast(FP8X4),
+                scales=v_scales[:, cols],
+                in_=v_grouped[w][:, cols, :].rearrange("p c j -> p (c j)"),
             )
 
-        def layer_norm(w, i, y, y_sum):
-            neg_mean = stats.tile([P, 1], F32)
-            nc.vector.tensor_scalar(
-                out=neg_mean[:], in0=y_sum[:, 0:1], scalar1=y_sum[:, 1:2], scalar2=-1.0 / FEATURES, op0=ALU.add, op1=ALU.mult
-            )
-            squares = stage.tile([P, FEATURES], BF16)
-            sum_sq = stats.tile([P, 1], F32)
-            nc.scalar.activation(out=squares[:], in_=y[:], func=ACT.Square, bias=neg_mean[:], scale=1.0, accum_out=sum_sq[:])
-            z = rows.tile([P, FEATURES], F32)
-            nc.vector.scalar_tensor_tensor(out=z[:], in0=y[:], scalar=neg_mean[:], in1=gain[:], op0=ALU.add, op1=ALU.mult)
-            std = stats.tile([P, 1], F32)
-            nc.scalar.activation(out=std[:], in_=sum_sq[:], func=ACT.Sqrt, bias=eps[:], scale=1.0 / FEATURES)
+        def pool_half(w, h):
+            v_codes, v_scales = v_mx[w]
+            cols = slice(h * HALF, (h + 1) * HALF)
+            for i in range(SLOT_TILES):
+                slots = slice(i * P, (i + 1) * P)
+                mem = psum_m.tile([P, HALF], F32, tag="m")
+                nc.tensor.matmul_mx(
+                    out=mem[:],
+                    lhsT=e_codes[:, w, slots].bitcast(FP8X4),
+                    lhsT_scale=e_scales[:, w, slots],
+                    rhs=v_codes[:, cols].bitcast(FP8X4),
+                    rhs_scale=v_scales[:, cols],
+                    start=True,
+                    stop=True,
+                )
+                nc.vector.scalar_tensor_tensor(
+                    out=y_rows[w, i][:, cols],
+                    in0=mem[:],
+                    scalar=inv_sum[:, w, i : i + 1],
+                    in1=slot_rows[w][:, i, cols],
+                    op0=ALU.mult,
+                    op1=ALU.add,
+                    accum_out=y_sums[w, i][:, h : h + 1],
+                )
+
+        neg_means = {}
+        stds = {}
+        z_rows = {}
+
+        def means(w):
+            for i in range(SLOT_TILES):
+                y_sum = y_sums[w, i]
+                neg_mean = stats.tile([P, 1], F32)
+                nc.vector.tensor_scalar(
+                    out=neg_mean[:], in0=y_sum[:, 0:1], scalar1=y_sum[:, 1:2], scalar2=-1.0 / FEATURES, op0=ALU.add, op1=ALU.mult
+                )
+                neg_means[w, i] = neg_mean
+
+        def deviations(w):
+            for i in range(SLOT_TILES):
+                y = y_rows[w, i]
+                neg_mean = neg_means[w, i]
+                squares = stage.tile([P, FEATURES], BF16)
+                sum_sq = stats.tile([P, 1], F32)
+                nc.scalar.activation(out=squares[:], in_=y[:], func=ACT.Square, bias=neg_mean[:], scale=1.0, accum_out=sum_sq[:])
+                std = stats.tile([P, 1], F32)
+                nc.scalar.activation(out=std[:], in_=sum_sq[:], func=ACT.Sqrt, bias=eps[:], scale=1.0 / FEATURES)
+                z = rows.tile([P, FEATURES], F32)
+                nc.vector.scalar_tensor_tensor(out=z[:], in0=y[:], scalar=neg_mean[:], in1=gain[:], op0=ALU.add, op1=ALU.mult)
+                stds[w, i] = std
+                z_rows[w, i] = z
+
+        def finish(w, i):
+            z = z_rows[w, i]
             inv_std = stats.tile([P, 1], F32)
-            nc.vector.reciprocal(out=inv_std[:], in_=std[:])
+            nc.vector.reciprocal(out=inv_std[:], in_=stds[w, i][:])
             nc.vector.scalar_tensor_tensor(out=z[:], in0=z[:], scalar=inv_std[:], in1=shift[:], op0=ALU.mult, op1=ALU.add)
             nc.sync.dma_start(out=out[w].rearrange("(p i) d -> p i d", i=SLOT_TILES)[:, i, :], in_=z[:])
 
         for w in range(CLASSES):
             softmax_numerators(w)
-        for w in range(CLASSES):
+        transpose_e(0)
+        transpose_e(1)
+        transpose_flat(0)
+        quantise_e(0)
+        quantise_e(1)
+        quantise_flat(0)
+        for w in range(M_BANKS, CLASSES):
+            first = (w - M_BANKS) * WV_RUN
+            for c in range(first, first + WV_RUN):
+                transpose_wv(c)
+            transpose_e(w)
+            quantise_wv(first, WV_RUN)
             quantise_e(w)
-        flat_mx = {0: quantise_flat(0)}
-        for c in range(OUT_TILES):
-            quantise_wv(c)
-        for w in range(CLASSES):
-            flat_codes, flat_scales = flat_mx[w]
-            v_grouped = stage.tile([P, FEATURES, PACK], BF16, align_bytes=64)
-            v_codes = stage.tile([P, FEATURES], U32, align_bytes=64)
-            v_scales = stage.tile([P, FEATURES], U8, align_bytes=64)
-            y_rows = [rows.tile([P, FEATURES], F32, name="y") for i in range(SLOT_TILES)]
-            y_sums = [stats.tile([P, HALVES], F32, name="y_sum") for i in range(SLOT_TILES)]
-            for h in range(HALVES):
-                for c in range(h * OUT_TILES // HALVES, (h + 1) * OUT_TILES // HALVES):
-                    project(flat_codes, flat_scales, c, v_grouped)
-                if h == 0 and w + 1 < CLASSES:
-                    flat_mx[w + 1] = quantise_flat(w + 1)
-                cols = slice(h * HALF, (h + 1) * HALF)
-                nc.vector.quantize_mx(
-                    out=v_codes[:, cols].bitcast(FP8X4),
-                    scales=v_scales[:, cols],
-                    in_=v_grouped[:, cols, :].rearrange("p c j -> p (c j)"),
-                )
-                for i in range(SLOT_TILES):
-                    pool_half(w, i, h, v_codes, v_scales, y_rows[i], y_sums[i])
-            for i in range(SLOT_TILES):
-                layer_norm(w, i, y_rows[i], y_sums[i])
+
+        def live(w):
+            return 0 <= w < CLASSES
+
+        for w in range(CLASSES + 2):
+            if live(w):
+                open_class(w)
+            if live(w - 1):
+                quantise_v(w - 1, 1)
+            if live(w - 2):
+                finish(w - 2, 1)
+            if live(w):
+                for c in range(0, OUT_TILES // 2):
+                    project(w, c)
+            if live(w - 1):
+                pool_half(w - 1, 1)
+                means(w - 1)
+            if live(w + 1):
+                transpose_flat(w + 1)
+            if live(w - 1):
+                deviations(w - 1)
+            if live(w):
+                for c in range(OUT_TILES // 2, OUT_TILES):
+                    project(w, c)
+                quantise_v(w, 0)
+            if live(w + 1):
+                quantise_flat(w + 1)
+            if live(w - 1):
+                finish(w - 1, 0)
+            if live(w):
+                pool_half(w, 0)

@@ -89,6 +89,8 @@ def tile_consensustransportmemorypool_pb_kernel(
         make_identity(nc, ident_bf16[:])
         eps = consts.tile([P, 1], F32)
         nc.vector.memset(eps[:], LN_EPS)
+        warm = consts.tile([P, 1], F32)
+        nc.scalar.activation(out=warm[:], in_=eps[:], func=ACT.Exp)
 
         neg_max = keep.tile([P, CLASSES, SLOT_TILES], F32)
         e_sum = keep.tile([P, CLASSES, SLOT_TILES], F32)
@@ -99,7 +101,10 @@ def tile_consensustransportmemorypool_pb_kernel(
         e_banks = {}
 
         def softmax_numerators(w):
-            nc.vector.tensor_reduce(out=neg_max[:, w, :], in_=logit_rows[:, w], axis=AXIS.X, op=ALU.max, negate=True)
+            for i in range(SLOT_TILES):
+                nc.vector.tensor_reduce(
+                    out=neg_max[:, w, i : i + 1], in_=logit_rows[:, w, i, :], axis=AXIS.X, op=ALU.max, negate=True
+                )
             for i in range(SLOT_TILES):
                 nc.scalar.activation(
                     out=e_rows[:, w, i, :],
@@ -288,33 +293,39 @@ def tile_consensustransportmemorypool_pb_kernel(
             quantise_wv(first, WV_RUN)
             quantise_e(w)
 
+        FIRST_HALF = range(0, OUT_TILES // 2)
+        SECOND_HALF = range(OUT_TILES // 2, OUT_TILES)
+
         def live(w):
             return 0 <= w < CLASSES
 
+        transpose_flat(1)
+        open_class(0)
+        for c in FIRST_HALF:
+            project(0, c)
         for w in range(CLASSES + 2):
-            if live(w):
-                open_class(w)
             if live(w - 1):
                 quantise_v(w - 1, 1)
             if live(w - 2):
                 finish(w - 2, 1)
-            if live(w):
-                for c in range(0, OUT_TILES // 2):
-                    project(w, c)
-            if live(w - 1):
-                pool_half(w - 1, 1)
-                means(w - 1)
-            if live(w + 1):
-                transpose_flat(w + 1)
-            if live(w - 1):
-                deviations(w - 1)
-            if live(w):
-                for c in range(OUT_TILES // 2, OUT_TILES):
-                    project(w, c)
-                quantise_v(w, 0)
             if live(w + 1):
                 quantise_flat(w + 1)
             if live(w - 1):
-                finish(w - 1, 0)
+                pool_half(w - 1, 1)
+                means(w - 1)
+            if live(w):
+                for c in SECOND_HALF:
+                    project(w, c)
+                quantise_v(w, 0)
+            if live(w - 1):
+                deviations(w - 1)
             if live(w):
                 pool_half(w, 0)
+            if live(w - 1):
+                finish(w - 1, 0)
+            if live(w + 2):
+                transpose_flat(w + 2)
+            if live(w + 1):
+                open_class(w + 1)
+                for c in FIRST_HALF:
+                    project(w + 1, c)

@@ -74,12 +74,12 @@ def tile_consensustransportmemorypool_pb_kernel(
         for c in range(0, OUT_TILES, 2):
             nc.sync.dma_start(out=wv_rows_by_tile[:, c : c + 2, :], in_=wv_tiles[:, c : c + 2, :])
         load_flat(1)
+        load_flat(2)
         load_slots(0)
         nc.sync.dma_start(out=gain[:], in_=g_out.partition_broadcast(P))
         nc.sync.dma_start(out=shift[:], in_=b_out.partition_broadcast(P))
-        load_flat(2)
-        load_slots(1)
         load_flat(3)
+        load_slots(1)
         load_slots(2)
         load_slots(3)
 

@@ -43,8 +43,8 @@ def tile_consensustransportmemorypool_pb_kernel(
         inputs = stack.enter_context(tc.tile_pool(name="inputs", bufs=1))
         keep = stack.enter_context(tc.tile_pool(name="keep", bufs=1))
         stage = stack.enter_context(tc.tile_pool(name="stage", bufs=2))
-        rows = stack.enter_context(tc.tile_pool(name="rows", bufs=4))
-        stats = stack.enter_context(tc.tile_pool(name="stats", bufs=4))
+        rows = stack.enter_context(tc.tile_pool(name="rows", bufs=6))
+        stats = stack.enter_context(tc.tile_pool(name="stats", bufs=6))
         psum_s = stack.enter_context(tc.psum_pool(name="psum_s", bufs=S_BANKS))
         psum_m = stack.enter_context(tc.psum_pool(name="psum_m", bufs=M_BANKS))
         stack.enter_context(tc.manual_schedule())
@@ -85,12 +85,12 @@ def tile_consensustransportmemorypool_pb_kernel(
 
         ident_f32 = consts.tile([P, P], F32)
         make_identity(nc, ident_f32[:])
-        ident_bf16 = consts.tile([P, P], BF16)
-        make_identity(nc, ident_bf16[:])
-        eps = consts.tile([P, 1], F32)
-        nc.vector.memset(eps[:], LN_EPS)
+        zero = consts.tile([P, 1], F32)
+        nc.vector.memset(zero[:], 0.0)
+        minus_half = consts.tile([P, 1], F32)
+        nc.gpsimd.memset(minus_half[:], -0.5)
         warm = consts.tile([P, 1], F32)
-        nc.scalar.activation(out=warm[:], in_=eps[:], func=ACT.Exp)
+        nc.scalar.activation(out=warm[:], in_=zero[:], func=ACT.Exp)
 
         neg_max = keep.tile([P, CLASSES, SLOT_TILES], F32)
         e_sum = keep.tile([P, CLASSES, SLOT_TILES], F32)
@@ -98,13 +98,27 @@ def tile_consensustransportmemorypool_pb_kernel(
         e_rows = keep.tile([P, CLASSES, SLOT_TILES, TOKENS], BF16)
         e_codes = keep.tile([P, CLASSES, SLOTS], U32, align_bytes=64)
         e_scales = keep.tile([P, CLASSES, SLOTS], U8, align_bytes=64)
-        e_banks = {}
 
-        def softmax_numerators(w):
+        def row_max(first, count):
+            classes = slice(first, first + count)
+            l = logit_rows[:, classes].rearrange("p w i t -> p (w i) t")
+            halves = stage.tile([P, count * SLOT_TILES, TOKENS // 2], BF16, name="halves%d" % count)
+            nc.vector.tensor_tensor(out=halves[:], in0=l[:, :, : TOKENS // 2], in1=l[:, :, TOKENS // 2 :], op=ALU.max)
+            quarters = stage.tile([P, count * SLOT_TILES, TOKENS // 4], BF16, name="quarters%d" % count)
+            nc.vector.tensor_tensor(
+                out=quarters[:], in0=halves[:, :, : TOKENS // 4], in1=halves[:, :, TOKENS // 4 :], op=ALU.max
+            )
+            nc.vector.tensor_reduce(
+                out=neg_max[:, classes].rearrange("p w i -> p (w i)"), in_=quarters[:], axis=AXIS.X, op=ALU.max, negate=True
+            )
+
+        def first_row_max():
             for i in range(SLOT_TILES):
                 nc.vector.tensor_reduce(
-                    out=neg_max[:, w, i : i + 1], in_=logit_rows[:, w, i, :], axis=AXIS.X, op=ALU.max, negate=True
+                    out=neg_max[:, 0, i : i + 1], in_=logit_rows[:, 0, i, :], axis=AXIS.X, op=ALU.max, negate=True
                 )
+
+        def exponentials(w):
             for i in range(SLOT_TILES):
                 nc.scalar.activation(
                     out=e_rows[:, w, i, :],
@@ -115,31 +129,39 @@ def tile_consensustransportmemorypool_pb_kernel(
                     accum_out=e_sum[:, w, i : i + 1],
                 )
 
+        e_groups = {}
+
         def transpose_e(w):
-            e_t = psum_m.tile([P, PACK, SLOTS], BF16, tag="m")
+            e_t = psum_m.tile([P, 2, SLOTS], F32, tag="m")
             for i in range(SLOT_TILES):
-                every_fourth = e_rows[:, w, i, :].rearrange("s (p j) -> s j p", j=PACK)
-                for j in range(PACK):
-                    nc.tensor.transpose(e_t[:, j, i * P : (i + 1) * P], every_fourth[:, j, :], ident_bf16[:])
-            e_banks[w] = e_t
+                words = e_rows[:, w, i, :].bitcast(F32)
+                for u in range(2):
+                    nc.tensor.transpose(e_t[:, u, i * P : (i + 1) * P], words[:, u::2], ident_f32[:])
+            e_grouped = stage.tile([P, SLOTS, PACK], BF16, align_bytes=64)
+            nc.vector.tensor_copy(
+                out=e_grouped[:].rearrange("p s j -> p (s j)").bitcast(F32).rearrange("p (s u) -> p s u", u=2),
+                in_=e_t[:].rearrange("p u s -> p s u"),
+            )
+            e_groups[w] = e_grouped
 
         def quantise_e(w):
-            e_grouped = stage.tile([P, SLOTS, PACK], BF16, align_bytes=64)
-            nc.vector.tensor_copy(out=e_grouped[:], in_=e_banks[w][:].rearrange("p j s -> p s j"))
-            nc.vector.reciprocal(out=inv_sum[:, w, :], in_=e_sum[:, w, :])
             nc.vector.quantize_mx(
                 out=e_codes[:, w, :].bitcast(FP8X4),
                 scales=e_scales[:, w, :],
-                in_=e_grouped[:].rearrange("p s j -> p (s j)"),
+                in_=e_groups[w][:].rearrange("p s j -> p (s j)"),
             )
 
-        def transpose_row_tile(words, grouped_words):
-            x_t = psum_s.tile([P, K_PASSES, 2, P], F32, tag="s")
+        def transpose_row_tile(words, grouped_words, by_vector=False):
+            if by_vector:
+                x_t = psum_m.tile([P, K_PASSES, 2, P], F32, tag="m")
+            else:
+                x_t = psum_s.tile([P, K_PASSES, 2, P], F32, tag="s")
             for g in range(K_PASSES):
                 for u in range(2):
                     first = (2 * g + u) * P
                     nc.tensor.transpose(x_t[:, g, u, :], words[:, first : first + P], ident_f32[:])
-            nc.scalar.copy(
+            copy = nc.vector.tensor_copy if by_vector else nc.scalar.copy
+            copy(
                 out=grouped_words.rearrange("p (g r u) -> p g r u", g=K_PASSES, u=2),
                 in_=x_t[:].rearrange("p g u r -> p g r u"),
             )
@@ -152,7 +174,8 @@ def tile_consensustransportmemorypool_pb_kernel(
             words = flat_rows[w][:].bitcast(F32)
             grouped_words = flat_grouped[w][:].bitcast(F32)
             for j in range(PACK):
-                transpose_row_tile(words[:, j * WORDS : (j + 1) * WORDS], grouped_words[:, j * WORDS : (j + 1) * WORDS])
+                tile = slice(j * WORDS, (j + 1) * WORDS)
+                transpose_row_tile(words[:, tile], grouped_words[:, tile], w == 0 and j >= 2)
 
         def quantise_flat(w):
             flat_codes = stage.tile([P, PACK * K_PASSES * P], U32, align_bytes=64)
@@ -168,7 +191,8 @@ def tile_consensustransportmemorypool_pb_kernel(
         def transpose_wv(c):
             words = wv_rows[:].bitcast(F32)
             grouped_words = wv_grouped[:].bitcast(F32)
-            transpose_row_tile(words[:, c * WORDS : (c + 1) * WORDS], grouped_words[:, c * WORDS : (c + 1) * WORDS])
+            tile = slice(c * WORDS, (c + 1) * WORDS)
+            transpose_row_tile(words[:, tile], grouped_words[:, tile], c % WV_RUN == WV_RUN - 1)
 
         def quantise_wv(first, count):
             nc.vector.quantize_mx(
@@ -244,49 +268,65 @@ def tile_consensustransportmemorypool_pb_kernel(
                 )
 
         neg_means = {}
-        stds = {}
+        inv_stds = {}
         z_rows = {}
 
         def means(w):
             for i in range(SLOT_TILES):
                 y_sum = y_sums[w, i]
                 neg_mean = stats.tile([P, 1], F32)
-                nc.vector.tensor_scalar(
-                    out=neg_mean[:], in0=y_sum[:, 0:1], scalar1=y_sum[:, 1:2], scalar2=-1.0 / FEATURES, op0=ALU.add, op1=ALU.mult
+                parts = stats.tile([P, HALVES], F32)
+                nc.scalar.activation(
+                    out=parts[:], in_=y_sum[:], func=ACT.Identity, scale=-1.0 / FEATURES, accum_out=neg_mean[:]
                 )
                 neg_means[w, i] = neg_mean
 
-        def deviations(w):
-            for i in range(SLOT_TILES):
-                y = y_rows[w, i]
-                neg_mean = neg_means[w, i]
-                squares = stage.tile([P, FEATURES], BF16)
-                sum_sq = stats.tile([P, 1], F32)
-                nc.scalar.activation(out=squares[:], in_=y[:], func=ACT.Square, bias=neg_mean[:], scale=1.0, accum_out=sum_sq[:])
-                std = stats.tile([P, 1], F32)
-                nc.scalar.activation(out=std[:], in_=sum_sq[:], func=ACT.Sqrt, bias=eps[:], scale=1.0 / FEATURES)
-                z = rows.tile([P, FEATURES], F32)
-                nc.vector.scalar_tensor_tensor(out=z[:], in0=y[:], scalar=neg_mean[:], in1=gain[:], op0=ALU.add, op1=ALU.mult)
-                stds[w, i] = std
-                z_rows[w, i] = z
+        def squares_of(w, i):
+            squares = stage.tile([P, FEATURES], BF16)
+            sum_sq = stats.tile([P, 1], F32)
+            nc.scalar.activation(
+                out=squares[:], in_=y_rows[w, i][:], func=ACT.Square, bias=neg_means[w, i][:], scale=1.0, accum_out=sum_sq[:]
+            )
+            var = stats.tile([P, 1], F32)
+            nc.gpsimd.tensor_scalar(
+                out=var[:], in0=sum_sq[:], scalar1=1.0 / FEATURES, scalar2=LN_EPS, op0=ALU.mult, op1=ALU.add
+            )
+            inv_std = stats.tile([P, 1], F32)
+            nc.gpsimd.tensor_tensor(out=inv_std[:], in0=var[:], in1=minus_half[:], op=ALU.pow)
+            inv_stds[w, i] = inv_std
+
+        def centre(w, i):
+            z = rows.tile([P, FEATURES], F32)
+            nc.vector.scalar_tensor_tensor(
+                out=z[:], in0=y_rows[w, i][:], scalar=neg_means[w, i][:], in1=gain[:], op0=ALU.add, op1=ALU.mult
+            )
+            z_rows[w, i] = z
 
         def finish(w, i):
             z = z_rows[w, i]
-            inv_std = stats.tile([P, 1], F32)
-            nc.vector.reciprocal(out=inv_std[:], in_=stds[w, i][:])
-            nc.vector.scalar_tensor_tensor(out=z[:], in0=z[:], scalar=inv_std[:], in1=shift[:], op0=ALU.mult, op1=ALU.add)
-            nc.sync.dma_start(out=out[w].rearrange("(p i) d -> p i d", i=SLOT_TILES)[:, i, :], in_=z[:])
+            out_rows = out[w].rearrange("(p i) d -> p i d", i=SLOT_TILES)
+            width = FEATURES // 2 if (w, i) == (CLASSES - 1, SLOT_TILES - 1) else FEATURES
+            for first in range(0, FEATURES, width):
+                cols = slice(first, first + width)
+                nc.vector.scalar_tensor_tensor(
+                    out=z[:, cols], in0=z[:, cols], scalar=inv_stds[w, i][:], in1=shift[:, cols], op0=ALU.mult, op1=ALU.add
+                )
+                nc.sync.dma_start(out=out_rows[:, i, cols], in_=z[:, cols])
 
+        first_row_max()
+        row_max(1, 1)
+        row_max(2, 2)
         for w in range(CLASSES):
-            softmax_numerators(w)
+            exponentials(w)
         transpose_e(0)
         transpose_e(1)
         transpose_flat(0)
         quantise_e(0)
         quantise_e(1)
         quantise_flat(0)
-        for w in range(M_BANKS, CLASSES):
-            first = (w - M_BANKS) * WV_RUN
+        nc.vector.reciprocal(out=inv_sum[:], in_=e_sum[:])
+        for w in range(2, CLASSES):
+            first = (w - 2) * WV_RUN
             for c in range(first, first + WV_RUN):
                 transpose_wv(c)
             transpose_e(w)
@@ -307,24 +347,28 @@ def tile_consensustransportmemorypool_pb_kernel(
             if live(w - 1):
                 quantise_v(w - 1, 1)
             if live(w - 2):
-                finish(w - 2, 1)
+                finish(w - 2, 0)
             if live(w + 1):
                 quantise_flat(w + 1)
             if live(w - 1):
                 pool_half(w - 1, 1)
                 means(w - 1)
+            if live(w - 2):
+                finish(w - 2, 1)
             if live(w):
                 for c in SECOND_HALF:
                     project(w, c)
                 quantise_v(w, 0)
             if live(w - 1):
-                deviations(w - 1)
+                squares_of(w - 1, 0)
+                for i in range(SLOT_TILES):
+                    centre(w - 1, i)
             if live(w):
                 pool_half(w, 0)
-            if live(w - 1):
-                finish(w - 1, 0)
             if live(w + 2):
                 transpose_flat(w + 2)
+            if live(w - 1):
+                squares_of(w - 1, 1)
             if live(w + 1):
                 open_class(w + 1)
                 for c in FIRST_HALF:

@@ -27,8 +27,8 @@ OUT_TILES = FEATURES // P
 HALF = 512
 HALVES = FEATURES // HALF
 
-S_BANKS = 6
-M_BANKS = 2
+S_BANKS = 5
+M_BANKS = 3
 WV_RUN = 4
 
 FLOPS = 2 * CLASSES * TOKENS * FEATURES * FEATURES + 2 * CLASSES * SLOTS * TOKENS * FEATURES
@@ -137,18 +137,20 @@ def tile_consensustransportmemorypool_pb_kernel(
                 words = e_rows[:, w, i, :].bitcast(F32)
                 for u in range(2):
                     nc.tensor.transpose(e_t[:, u, i * P : (i + 1) * P], words[:, u::2], ident_f32[:])
-            e_grouped = stage.tile([P, SLOTS, PACK], BF16, align_bytes=64)
+            pair, member = divmod(w, 2)
+            if member == 0:
+                e_groups[pair] = stage.tile([P, 2, SLOTS, PACK], BF16, align_bytes=64, name="e_grouped")
             nc.vector.tensor_copy(
-                out=e_grouped[:].rearrange("p s j -> p (s j)").bitcast(F32).rearrange("p (s u) -> p s u", u=2),
+                out=e_groups[pair][:, member].rearrange("p s j -> p (s j)").bitcast(F32).rearrange("p (s u) -> p s u", u=2),
                 in_=e_t[:].rearrange("p u s -> p s u"),
             )
-            e_groups[w] = e_grouped
 
-        def quantise_e(w):
+        def quantise_e(pair):
+            classes = slice(2 * pair, 2 * pair + 2)
             nc.vector.quantize_mx(
-                out=e_codes[:, w, :].bitcast(FP8X4),
-                scales=e_scales[:, w, :],
-                in_=e_groups[w][:].rearrange("p s j -> p (s j)"),
+                out=e_codes[:, classes, :].rearrange("p w s -> p (w s)").bitcast(FP8X4),
+                scales=e_scales[:, classes, :].rearrange("p w s -> p (w s)"),
+                in_=e_groups[pair][:].rearrange("p w s j -> p (w s j)"),
             )
 
         def transpose_row_tile(words, grouped_words, by_vector=False):
@@ -175,7 +177,7 @@ def tile_consensustransportmemorypool_pb_kernel(
             grouped_words = flat_grouped[w][:].bitcast(F32)
             for j in range(PACK):
                 tile = slice(j * WORDS, (j + 1) * WORDS)
-                transpose_row_tile(words[:, tile], grouped_words[:, tile], w == 0 and j >= 2)
+                transpose_row_tile(words[:, tile], grouped_words[:, tile], (w == 0 and j >= 2) or (w == 1 and j == 3))
 
         def quantise_flat(w):
             flat_codes = stage.tile([P, PACK * K_PASSES * P], U32, align_bytes=64)
@@ -192,7 +194,7 @@ def tile_consensustransportmemorypool_pb_kernel(
             words = wv_rows[:].bitcast(F32)
             grouped_words = wv_grouped[:].bitcast(F32)
             tile = slice(c * WORDS, (c + 1) * WORDS)
-            transpose_row_tile(words[:, tile], grouped_words[:, tile], c % WV_RUN == WV_RUN - 1)
+            transpose_row_tile(words[:, tile], grouped_words[:, tile])
 
         def quantise_wv(first, count):
             nc.vector.quantize_mx(
@@ -314,7 +316,7 @@ def tile_consensustransportmemorypool_pb_kernel(
                 nc.sync.dma_start(out=out_rows[:, i, cols], in_=z[:, cols])
 
         first_row_max()
-        row_max(1, 1)
+        nc.vector.tensor_reduce(out=neg_max[:, 1, :], in_=logit_rows[:, 1], axis=AXIS.X, op=ALU.max, negate=True)
         row_max(2, 2)
         for w in range(CLASSES):
             exponentials(w)
@@ -322,7 +324,6 @@ def tile_consensustransportmemorypool_pb_kernel(
         transpose_e(1)
         transpose_flat(0)
         quantise_e(0)
-        quantise_e(1)
         quantise_flat(0)
         nc.vector.reciprocal(out=inv_sum[:], in_=e_sum[:])
         for w in range(2, CLASSES):
@@ -331,7 +332,7 @@ def tile_consensustransportmemorypool_pb_kernel(
                 transpose_wv(c)
             transpose_e(w)
             quantise_wv(first, WV_RUN)
-            quantise_e(w)
+        quantise_e(1)
 
         FIRST_HALF = range(0, OUT_TILES // 2)
         SECOND_HALF = range(OUT_TILES // 2, OUT_TILES)

@@ -177,7 +177,7 @@ def tile_consensustransportmemorypool_pb_kernel(
             grouped_words = flat_grouped[w][:].bitcast(F32)
             for j in range(PACK):
                 tile = slice(j * WORDS, (j + 1) * WORDS)
-                transpose_row_tile(words[:, tile], grouped_words[:, tile], (w == 0 and j >= 2) or (w == 1 and j == 3))
+                transpose_row_tile(words[:, tile], grouped_words[:, tile], w == 0 and j == 3)
 
         def quantise_flat(w):
             flat_codes = stage.tile([P, PACK * K_PASSES * P], U32, align_bytes=64)
@@ -316,7 +316,7 @@ def tile_consensustransportmemorypool_pb_kernel(
                 nc.sync.dma_start(out=out_rows[:, i, cols], in_=z[:, cols])
 
         first_row_max()
-        nc.vector.tensor_reduce(out=neg_max[:, 1, :], in_=logit_rows[:, 1], axis=AXIS.X, op=ALU.max, negate=True)
+        row_max(1, 1)
         row_max(2, 2)
         for w in range(CLASSES):
             exponentials(w)

from contextlib import ExitStack

import concourse.mybir as mybir
from concourse.masks import make_identity

FP8X4 = mybir.dt.float8_e4m3fn_x4
BF16 = mybir.dt.bfloat16
F32 = mybir.dt.float32
U32 = mybir.dt.uint32
U8 = mybir.dt.uint8
ACT = mybir.ActivationFunctionType
ALU = mybir.AluOpType
AXIS = mybir.AxisListType

P = 128
PACK = 4
CLASSES = 4
SLOTS = 256
TOKENS = 512
FEATURES = 1024
LN_EPS = 1e-5

SLOT_TILES = SLOTS // P
K_PASSES = FEATURES // (P * PACK)
WORDS = FEATURES // 2
OUT_TILES = FEATURES // P
HALF = 512
HALVES = FEATURES // HALF

S_BANKS = 5
M_BANKS = 3
WV_RUN = 4

FLOPS = 2 * CLASSES * TOKENS * FEATURES * FEATURES + 2 * CLASSES * SLOTS * TOKENS * FEATURES


def tile_consensustransportmemorypool_pb_kernel(
    tc, logits, support_transport, Wv, class_slots, g_out, b_out, out
):
    nc = tc.nc
    with ExitStack() as stack:
        consts = stack.enter_context(tc.tile_pool(name="consts", bufs=1))
        inputs = stack.enter_context(tc.tile_pool(name="inputs", bufs=1))
        keep = stack.enter_context(tc.tile_pool(name="keep", bufs=1))
        stage = stack.enter_context(tc.tile_pool(name="stage", bufs=2))
        rows = stack.enter_context(tc.tile_pool(name="rows", bufs=6))
        stats = stack.enter_context(tc.tile_pool(name="stats", bufs=6))
        psum_s = stack.enter_context(tc.psum_pool(name="psum_s", bufs=S_BANKS))
        psum_m = stack.enter_context(tc.psum_pool(name="psum_m", bufs=M_BANKS))
        stack.enter_context(tc.manual_schedule())

        logit_rows = inputs.tile([P, CLASSES, SLOT_TILES, TOKENS], BF16)
        flat_rows = [inputs.tile([P, PACK * FEATURES], BF16, name="flat_rows%d" % w) for w in range(CLASSES)]
        wv_rows = inputs.tile([P, OUT_TILES * FEATURES], BF16)
        slot_rows = [inputs.tile([P, SLOT_TILES, FEATURES], BF16, name="slot_rows%d" % w) for w in range(CLASSES)]
        gain = consts.tile([P, FEATURES], BF16)
        shift = consts.tile([P, FEATURES], BF16)

        def load_flat(w):
            tokens = support_transport[w].rearrange("k t d -> (k t) d")
            nc.sync.dma_start(
                out=flat_rows[w][:].rearrange("p (j d) -> p j d", j=PACK),
                in_=tokens.rearrange("(p j) d -> p j d", j=PACK),
            )

        def load_slots(w):
            nc.sync.dma_start(out=slot_rows[w][:], in_=class_slots[w].rearrange("(p i) d -> p i d", i=SLOT_TILES))

        for w in range(CLASSES):
            nc.sync.dma_start(out=logit_rows[:, w], in_=logits[w].rearrange("(p i) t -> p i t", i=SLOT_TILES))
        load_flat(0)
        wv_tiles = Wv.rearrange("(c p) k -> p c k", p=P)
        wv_rows_by_tile = wv_rows[:].rearrange("p (c k) -> p c k", c=OUT_TILES)
        for c in range(0, OUT_TILES, 2):
            nc.sync.dma_start(out=wv_rows_by_tile[:, c : c + 2, :], in_=wv_tiles[:, c : c + 2, :])
        load_flat(1)
        load_flat(2)
        load_slots(0)
        nc.sync.dma_start(out=gain[:], in_=g_out.partition_broadcast(P))
        nc.sync.dma_start(out=shift[:], in_=b_out.partition_broadcast(P))
        load_flat(3)
        load_slots(1)
        load_slots(2)
        load_slots(3)

        ident_f32 = consts.tile([P, P], F32)
        make_identity(nc, ident_f32[:])
        zero = consts.tile([P, 1], F32)
        nc.vector.memset(zero[:], 0.0)
        minus_half = consts.tile([P, 1], F32)
        nc.gpsimd.memset(minus_half[:], -0.5)
        warm = consts.tile([P, 1], F32)
        nc.scalar.activation(out=warm[:], in_=zero[:], func=ACT.Exp)

        neg_max = keep.tile([P, CLASSES, SLOT_TILES], F32)
        e_sum = keep.tile([P, CLASSES, SLOT_TILES], F32)
        inv_sum = keep.tile([P, CLASSES, SLOT_TILES], F32)
        e_rows = keep.tile([P, CLASSES, SLOT_TILES, TOKENS], BF16)
        e_codes = keep.tile([P, CLASSES, SLOTS], U32, align_bytes=64)
        e_scales = keep.tile([P, CLASSES, SLOTS], U8, align_bytes=64)

        def row_max(first, count):
            classes = slice(first, first + count)
            l = logit_rows[:, classes].rearrange("p w i t -> p (w i) t")
            halves = stage.tile([P, count * SLOT_TILES, TOKENS // 2], BF16, name="halves%d" % count)
            nc.vector.tensor_tensor(out=halves[:], in0=l[:, :, : TOKENS // 2], in1=l[:, :, TOKENS // 2 :], op=ALU.max)
            quarters = stage.tile([P, count * SLOT_TILES, TOKENS // 4], BF16, name="quarters%d" % count)
            nc.vector.tensor_tensor(
                out=quarters[:], in0=halves[:, :, : TOKENS // 4], in1=halves[:, :, TOKENS // 4 :], op=ALU.max
            )
            nc.vector.tensor_reduce(
                out=neg_max[:, classes].rearrange("p w i -> p (w i)"), in_=quarters[:], axis=AXIS.X, op=ALU.max, negate=True
            )

        def first_row_max():
            for i in range(SLOT_TILES):
                nc.vector.tensor_reduce(
                    out=neg_max[:, 0, i : i + 1], in_=logit_rows[:, 0, i, :], axis=AXIS.X, op=ALU.max, negate=True
                )

        def exponentials(w):
            for i in range(SLOT_TILES):
                nc.scalar.activation(
                    out=e_rows[:, w, i, :],
                    in_=logit_rows[:, w, i, :],
                    func=ACT.Exp,
                    bias=neg_max[:, w, i : i + 1],
                    scale=1.0,
                    accum_out=e_sum[:, w, i : i + 1],
                )

        e_groups = {}

        def transpose_e(w):
            e_t = psum_m.tile([P, 2, SLOTS], F32, tag="m")
            for i in range(SLOT_TILES):
                words = e_rows[:, w, i, :].bitcast(F32)
                for u in range(2):
                    nc.tensor.transpose(e_t[:, u, i * P : (i + 1) * P], words[:, u::2], ident_f32[:])
            pair, member = divmod(w, 2)
            if member == 0:
                e_groups[pair] = stage.tile([P, 2, SLOTS, PACK], BF16, align_bytes=64, name="e_grouped")
            nc.vector.tensor_copy(
                out=e_groups[pair][:, member].rearrange("p s j -> p (s j)").bitcast(F32).rearrange("p (s u) -> p s u", u=2),
                in_=e_t[:].rearrange("p u s -> p s u"),
            )

        def quantise_e(pair):
            classes = slice(2 * pair, 2 * pair + 2)
            nc.vector.quantize_mx(
                out=e_codes[:, classes, :].rearrange("p w s -> p (w s)").bitcast(FP8X4),
                scales=e_scales[:, classes, :].rearrange("p w s -> p (w s)"),
                in_=e_groups[pair][:].rearrange("p w s j -> p (w s j)"),
            )

        def transpose_row_tile(words, grouped_words, by_vector=False):
            if by_vector:
                x_t = psum_m.tile([P, K_PASSES, 2, P], F32, tag="m")
            else:
                x_t = psum_s.tile([P, K_PASSES, 2, P], F32, tag="s")
            for g in range(K_PASSES):
                for u in range(2):
                    first = (2 * g + u) * P
                    nc.tensor.transpose(x_t[:, g, u, :], words[:, first : first + P], ident_f32[:])
            copy = nc.vector.tensor_copy if by_vector else nc.scalar.copy
            copy(
                out=grouped_words.rearrange("p (g r u) -> p g r u", g=K_PASSES, u=2),
                in_=x_t[:].rearrange("p g u r -> p g r u"),
            )

        flat_grouped = {}
        flat_mx = {}

        def transpose_flat(w):
            flat_grouped[w] = stage.tile([P, PACK * FEATURES], BF16, align_bytes=64, name="flat_grouped")
            words = flat_rows[w][:].bitcast(F32)
            grouped_words = flat_grouped[w][:].bitcast(F32)
            for j in range(PACK):
                tile = slice(j * WORDS, (j + 1) * WORDS)
                transpose_row_tile(words[:, tile], grouped_words[:, tile], w == 0 and j == 3)

        def quantise_flat(w):
            flat_codes = stage.tile([P, PACK * K_PASSES * P], U32, align_bytes=64)
            flat_scales = stage.tile([P, PACK * K_PASSES * P], U8, align_bytes=64)
            nc.vector.quantize_mx(out=flat_codes[:].bitcast(FP8X4), scales=flat_scales[:], in_=flat_grouped[w][:])
            flat_mx[w] = (flat_codes, flat_scales)

        wv_codes = keep.tile([P, OUT_TILES * K_PASSES * P], U32, align_bytes=64)
        wv_scales = keep.tile([P, OUT_TILES * K_PASSES * P], U8, align_bytes=64)

        wv_grouped = keep.tile([P, OUT_TILES * FEATURES], BF16, align_bytes=64)

        def transpose_wv(c):
            words = wv_rows[:].bitcast(F32)
            grouped_words = wv_grouped[:].bitcast(F32)
            tile = slice(c * WORDS, (c + 1) * WORDS)
            transpose_row_tile(words[:, tile], grouped_words[:, tile])

        def quantise_wv(first, count):
            nc.vector.quantize_mx(
                out=wv_codes[:, first * K_PASSES * P : (first + count) * K_PASSES * P].bitcast(FP8X4),
                scales=wv_scales[:, first * K_PASSES * P : (first + count) * K_PASSES * P],
                in_=wv_grouped[:, first * FEATURES : (first + count) * FEATURES],
            )

        v_grouped = {}
        v_mx = {}
        y_rows = {}
        y_sums = {}

        def open_class(w):
            v_grouped[w] = stage.tile([P, FEATURES, PACK], BF16, align_bytes=64, name="v_grouped")
            v_codes = stage.tile([P, FEATURES], U32, align_bytes=64)
            v_scales = stage.tile([P, FEATURES], U8, align_bytes=64)
            v_mx[w] = (v_codes, v_scales)
            for i in range(SLOT_TILES):
                y_rows[w, i] = rows.tile([P, FEATURES], F32, name="y")
                y_sums[w, i] = stats.tile([P, HALVES], F32, name="y_sum")

        def project(w, c):
            flat_codes, flat_scales = flat_mx[w]
            v_acc = psum_s.tile([P, PACK, P], F32, tag="s")
            for j in range(PACK):
                for g in range(K_PASSES):
                    tok = slice((j * K_PASSES + g) * P, (j * K_PASSES + g + 1) * P)
                    col = slice((c * K_PASSES + g) * P, (c * K_PASSES + g + 1) * P)
                    nc.tensor.matmul_mx(
                        out=v_acc[:, j, :],
                        lhsT=flat_codes[:, tok].bitcast(FP8X4),
                        lhsT_scale=flat_scales[:, tok],
                        rhs=wv_codes[:, col].bitcast(FP8X4),
                        rhs_scale=wv_scales[:, col],
                        start=(g == 0),
                        stop=(g == K_PASSES - 1),
                    )
            nc.scalar.copy(out=v_grouped[w][:, c * P : (c + 1) * P, :], in_=v_acc[:].rearrange("p j c -> p c j"))

        def quantise_v(w, h):
            v_codes, v_scales = v_mx[w]
            cols = slice(h * HALF, (h + 1) * HALF)
            nc.vector.quantize_mx(
                out=v_codes[:, cols].bitcast(FP8X4),
                scales=v_scales[:, cols],
                in_=v_grouped[w][:, cols, :].rearrange("p c j -> p (c j)"),
            )

        def pool_half(w, h):
            v_codes, v_scales = v_mx[w]
            cols = slice(h * HALF, (h + 1) * HALF)
            for i in range(SLOT_TILES):
                slots = slice(i * P, (i + 1) * P)
                mem = psum_m.tile([P, HALF], F32, tag="m")
                nc.tensor.matmul_mx(
                    out=mem[:],
                    lhsT=e_codes[:, w, slots].bitcast(FP8X4),
                    lhsT_scale=e_scales[:, w, slots],
                    rhs=v_codes[:, cols].bitcast(FP8X4),
                    rhs_scale=v_scales[:, cols],
                    start=True,
                    stop=True,
                )
                nc.vector.scalar_tensor_tensor(
                    out=y_rows[w, i][:, cols],
                    in0=mem[:],
                    scalar=inv_sum[:, w, i : i + 1],
                    in1=slot_rows[w][:, i, cols],
                    op0=ALU.mult,
                    op1=ALU.add,
                    accum_out=y_sums[w, i][:, h : h + 1],
                )

        neg_means = {}
        inv_stds = {}
        z_rows = {}

        def means(w):
            for i in range(SLOT_TILES):
                y_sum = y_sums[w, i]
                neg_mean = stats.tile([P, 1], F32)
                parts = stats.tile([P, HALVES], F32)
                nc.scalar.activation(
                    out=parts[:], in_=y_sum[:], func=ACT.Identity, scale=-1.0 / FEATURES, accum_out=neg_mean[:]
                )
                neg_means[w, i] = neg_mean

        def squares_of(w, i):
            squares = stage.tile([P, FEATURES], BF16)
            sum_sq = stats.tile([P, 1], F32)
            nc.scalar.activation(
                out=squares[:], in_=y_rows[w, i][:], func=ACT.Square, bias=neg_means[w, i][:], scale=1.0, accum_out=sum_sq[:]
            )
            var = stats.tile([P, 1], F32)
            nc.gpsimd.tensor_scalar(
                out=var[:], in0=sum_sq[:], scalar1=1.0 / FEATURES, scalar2=LN_EPS, op0=ALU.mult, op1=ALU.add
            )
            inv_std = stats.tile([P, 1], F32)
            nc.gpsimd.tensor_tensor(out=inv_std[:], in0=var[:], in1=minus_half[:], op=ALU.pow)
            inv_stds[w, i] = inv_std

        def centre(w, i):
            z = rows.tile([P, FEATURES], F32)
            nc.vector.scalar_tensor_tensor(
                out=z[:], in0=y_rows[w, i][:], scalar=neg_means[w, i][:], in1=gain[:], op0=ALU.add, op1=ALU.mult
            )
            z_rows[w, i] = z

        def finish(w, i):
            z = z_rows[w, i]
            out_rows = out[w].rearrange("(p i) d -> p i d", i=SLOT_TILES)
            width = FEATURES // 2 if (w, i) == (CLASSES - 1, SLOT_TILES - 1) else FEATURES
            for first in range(0, FEATURES, width):
                cols = slice(first, first + width)
                nc.vector.scalar_tensor_tensor(
                    out=z[:, cols], in0=z[:, cols], scalar=inv_stds[w, i][:], in1=shift[:, cols], op0=ALU.mult, op1=ALU.add
                )
                nc.sync.dma_start(out=out_rows[:, i, cols], in_=z[:, cols])

        first_row_max()
        row_max(1, 1)
        row_max(2, 2)
        for w in range(CLASSES):
            exponentials(w)
        transpose_e(0)
        transpose_e(1)
        transpose_flat(0)
        quantise_e(0)
        quantise_flat(0)
        nc.vector.reciprocal(out=inv_sum[:], in_=e_sum[:])
        for w in range(2, CLASSES):
            first = (w - 2) * WV_RUN
            for c in range(first, first + WV_RUN):
                transpose_wv(c)
            transpose_e(w)
            quantise_wv(first, WV_RUN)
        quantise_e(1)

        FIRST_HALF = range(0, OUT_TILES // 2)
        SECOND_HALF = range(OUT_TILES // 2, OUT_TILES)

        def live(w):
            return 0 <= w < CLASSES

        transpose_flat(1)
        open_class(0)
        for c in FIRST_HALF:
            project(0, c)
        for w in range(CLASSES + 2):
            if live(w - 1):
                quantise_v(w - 1, 1)
            if live(w - 2):
                finish(w - 2, 0)
            if live(w + 1):
                quantise_flat(w + 1)
            if live(w - 1):
                pool_half(w - 1, 1)
                means(w - 1)
            if live(w - 2):
                finish(w - 2, 1)
            if live(w):
                for c in SECOND_HALF:
                    project(w, c)
                quantise_v(w, 0)
            if live(w - 1):
                squares_of(w - 1, 0)
                for i in range(SLOT_TILES):
                    centre(w - 1, i)
            if live(w):
                pool_half(w, 0)
            if live(w + 2):
                transpose_flat(w + 2)
            if live(w - 1):
                squares_of(w - 1, 1)
            if live(w + 1):
                open_class(w + 1)
                for c in FIRST_HALF:
                    project(w + 1, c)
